import numpy as np
import ml_dtypes


def mxq(x, axis, fmt="e4m3"):
    dtype, down = {"e4m3": (ml_dtypes.float8_e4m3fn, 7), "e5m2": (ml_dtypes.float8_e5m2, 14)}[fmt]
    v = np.moveaxis(np.asarray(x, np.float32).astype(ml_dtypes.bfloat16).astype(np.float64), axis, -1)
    blocks = v.reshape(v.shape[:-1] + (-1, 32))
    amax = np.abs(blocks).max(-1, keepdims=True)
    byte = np.maximum(np.where(amax > 0, np.frexp(amax)[1] - 1 + 127, 0) - down, 1)
    scale = np.exp2(byte - 127.0)
    codes = (blocks / scale).astype(np.float32).astype(dtype).astype(np.float64)
    return np.moveaxis((codes * scale).reshape(v.shape), -1, axis)


WIDE = False


def mx_kscale(k):
    if not WIDE:
        return np.ones(k)
    levels = np.array([10, -10, 5, -5, 0])
    a = np.random.permutation(np.resize(levels, k // 512 * 4)).reshape(k // 512, 4)
    idx = np.arange(k)
    return np.exp2(a[idx // 512, idx % 128 // 32])


BF16 = ml_dtypes.bfloat16


def bf(x):
    return np.asarray(x, np.float32).astype(BF16)


def f64(x):
    return np.asarray(x).astype(np.float64)


B, S, A, D, V, KS, KM, KF = 4, 32, 16, 1024, 1024, 1024, 512, 512


def erf(v):
    z = np.clip(v, -6.0, 6.0)
    zz = 2.0 * z * z
    term = z.copy()
    total = z.copy()
    for n in range(1, 120):
        term = term * zz / (2.0 * n + 1.0)
        total = total + term
    return 2.0 / np.sqrt(np.pi) * np.exp(-z * z) * total


def gelu(v):
    return 0.5 * v * (1.0 + erf(v / np.sqrt(2.0)))


def sigmoid(v):
    return 1.0 / (1.0 + np.exp(-v))


def setup_inputs():
    s = mx_kscale(D)
    rn = np.random.standard_normal
    return {"hidden_states": bf(rn((B, S, D)) * s),
            "logits": bf(rn((B, S, V))),
            "W_f1": bf(rn((D, KF)) / np.sqrt(D) / s[:, None]),
            "b_f1": bf(rn(KF) * 0.5),
            "W_f2": bf(rn((KF, V)) * 2.5 / np.sqrt(KF)),
            "b_f2": bf(rn(V) * 0.5)}


def reference(hidden_states, logits, W_f1, b_f1, W_f2, b_f2):
    hid_f = gelu((mxq(f64(hidden_states), 2, "e4m3") @ mxq(f64(W_f1), 0, "e4m3")) + f64(b_f1))
    focus = sigmoid((mxq(hid_f, 2, "e4m3") @ mxq(f64(W_f2), 0, "e4m3")) + f64(b_f2))
    return f64(logits) * (1.0 + focus)

@@ -1,0 +1,200 @@
+from contextlib import ExitStack
+
+import concourse.mybir as mybir
+from concourse.masks import make_identity
+
+BF16 = mybir.dt.bfloat16
+F32 = mybir.dt.float32
+U32 = mybir.dt.uint32
+U8 = mybir.dt.uint8
+FP8X4 = mybir.dt.float8_e4m3fn_x4
+ACT = mybir.ActivationFunctionType
+ALU = mybir.AluOpType
+
+P = 128
+PACK = 4
+K_PASS = P * PACK
+D = 1024
+KF = 512
+V = 1024
+PIECE = 512
+RUN = 4
+VECTOR_COLS = 320
+
+FLOPS = 2 * P * D * KF + 2 * P * KF * V
+
+
+def regroup(nc, grouped, raw):
+    dst = grouped.rearrange("p (c i) j -> p c j i", i=RUN)
+    src = raw.rearrange("p j (c i) -> p c j i", i=RUN)
+    cut = VECTOR_COLS // RUN
+    nc.vector.tensor_copy(out=dst[:, :cut], in_=src[:, :cut])
+    nc.scalar.copy(out=dst[:, cut:], in_=src[:, cut:])
+
+
+def quantise(nc, codes, scales, grouped):
+    nc.vector.quantize_mx(
+        out=codes.bitcast(FP8X4),
+        scales=scales,
+        in_=grouped.rearrange("p w j -> p (w j)"),
+    )
+
+
+def tile_sparseoutputprojection_pb_s_kernel(
+    tc, hidden_states, logits, W_f1, b_f1, W_f2, b_f2, out
+):
+    nc = tc.nc
+    h_dram = hidden_states.flatten_outer_dims()
+    logits_dram = logits.flatten_outer_dims()
+    out_dram = out.flatten_outer_dims()
+    passes = D // K_PASS
+    w2_pieces = V // PIECE
+    chunks = PIECE // P
+
+    with ExitStack() as ctx:
+        keep = ctx.enter_context(tc.tile_pool(name="keep", bufs=1))
+        acc_pool = ctx.enter_context(tc.psum_pool(name="acc", bufs=4))
+        ps_pool = ctx.enter_context(tc.psum_pool(name="ps", bufs=1))
+
+        w1_raw = [keep.tile([P, PACK, KF], BF16, name="w1_raw%d" % g) for g in range(passes)]
+        w2_raw = [keep.tile([P, PACK, PIECE], BF16, name="w2_raw%d" % i) for i in range(w2_pieces)]
+        h_sb = keep.tile([P, D], BF16)
+        logits_sb = keep.tile([P, V], BF16)
+        w1_view = W_f1.rearrange("(g p j) c -> g p j c", p=P, j=PACK)
+        w2_view = W_f2.rearrange("(t p) n -> p t n", p=P)
+        nc.sync.dma_start(out=w1_raw[0][:], in_=w1_view[0])
+        nc.sync.dma_start(out=h_sb[:], in_=h_dram)
+        nc.sync.dma_start(out=w1_raw[1][:], in_=w1_view[1])
+        for i in range(w2_pieces):
+            nc.sync.dma_start(out=w2_raw[i][:], in_=w2_view[:, :, i * PIECE : (i + 1) * PIECE])
+        nc.sync.dma_start(out=logits_sb[:], in_=logits_dram)
+
+        bias_rows = keep.tile([P, P], BF16)
+        nc.vector.memset(bias_rows[:], 0.0)
+        nc.scalar.dma_start(out=bias_rows[0:4, :], in_=b_f1.rearrange("(t m) -> t m", m=P))
+        nc.scalar.dma_start(out=bias_rows[4:12, :], in_=b_f2.rearrange("(c m) -> c m", m=P))
+
+        warm_in = keep.tile([P, 1], F32)
+        warm_out = keep.tile([P, 1], F32)
+        nc.vector.memset(warm_in[:], 0.0)
+        nc.scalar.activation(out=warm_out[:], in_=warm_in[:], func=ACT.Gelu)
+
+        ident_f32 = keep.tile([P, P], F32)
+        ident_bf16 = keep.tile([P, P], BF16)
+        make_identity(nc, ident_f32[:])
+        make_identity(nc, ident_bf16[:])
+
+        w1_grouped = [
+            keep.tile([P, KF, PACK], BF16, align_bytes=64, name="w1_grouped%d" % g)
+            for g in range(passes)
+        ]
+        w1_codes = keep.tile([P, passes, KF], U32, align_bytes=64)
+        w1_scales = keep.tile([P, passes, KF], U8, align_bytes=64)
+        regroup(nc, w1_grouped[0][:], w1_raw[0][:])
+
+        bias_ps = ps_pool.tile([P, P], BF16)
+        nc.tensor.transpose(bias_ps[:], bias_rows[:], ident_bf16[:])
+        b1_col = keep.tile([P, 4], F32)
+        b2_half = keep.tile([P, 8], F32)
+        nc.vector.tensor_copy(out=b1_col[:], in_=bias_ps[:, 0:4])
+        nc.vector.tensor_scalar_mul(out=b2_half[:], in0=bias_ps[:, 4:12], scalar1=0.5)
+
+        h_words = h_sb[:].bitcast(F32).rearrange("r (g q u) -> r g u q", g=passes, u=2)
+        hT_ps = ps_pool.tile([P, passes, 2, P], F32)
+        for g in range(passes):
+            for u in range(2):
+                nc.tensor.transpose(hT_ps[:, g, u, :], h_words[:, g, u, :], ident_f32[:])
+        h_grouped = keep.tile([P, passes * P * PACK], BF16, align_bytes=64)
+        nc.scalar.copy(
+            out=h_grouped[:].bitcast(F32).rearrange("p (g r u) -> p g r u", g=passes, u=2),
+            in_=hT_ps[:].rearrange("p g u r -> p g r u"),
+        )
+        h_codes = keep.tile([P, passes, P], U32, align_bytes=64)
+        h_scales = keep.tile([P, passes, P], U8, align_bytes=64)
+
+        quantise(nc, w1_codes[:, 0, :], w1_scales[:, 0, :], w1_grouped[0][:])
+        nc.vector.quantize_mx(
+            out=h_codes[:].rearrange("p g r -> p (g r)").bitcast(FP8X4),
+            scales=h_scales[:].rearrange("p g r -> p (g r)"),
+            in_=h_grouped[:],
+        )
+
+        regroup(nc, w1_grouped[1][:], w1_raw[1][:])
+        quantise(nc, w1_codes[:, 1, :], w1_scales[:, 1, :], w1_grouped[1][:])
+
+        hid_ps = [acc_pool.tile([P, P], F32, tag="acc", name="hid_ps%d" % t) for t in range(PACK)]
+        for g in range(passes):
+            for t in range(PACK):
+                m_cols = slice(t * P, (t + 1) * P)
+                nc.tensor.matmul_mx(
+                    out=hid_ps[t][:],
+                    lhsT=w1_codes[:, g, m_cols].bitcast(FP8X4),
+                    lhsT_scale=w1_scales[:, g, m_cols],
+                    rhs=h_codes[:, g, :].bitcast(FP8X4),
+                    rhs_scale=h_scales[:, g, :],
+                    start=(g == 0),
+                    stop=(g == passes - 1),
+                )
+
+        w2_grouped = [
+            keep.tile([P, PIECE, PACK], BF16, align_bytes=64, name="w2_grouped%d" % i)
+            for i in range(w2_pieces)
+        ]
+        w2_codes = keep.tile([P, V], U32, align_bytes=64)
+        w2_scales = keep.tile([P, V], U8, align_bytes=64)
+        regroup(nc, w2_grouped[0][:], w2_raw[0][:])
+        quantise(nc, w2_codes[:, 0:PIECE], w2_scales[:, 0:PIECE], w2_grouped[0][:])
+
+        hid_planes = keep.tile([P, PACK, P], BF16)
+        for t in range(PACK):
+            nc.scalar.activation(
+                out=hid_planes[:, t, :], in_=hid_ps[t][:], func=ACT.Gelu,
+                bias=b1_col[:, t : t + 1], scale=1.0,
+            )
+        hid_grouped = keep.tile([P, P, PACK], BF16, align_bytes=64)
+        nc.vector.tensor_copy(
+            out=hid_grouped[:].rearrange("p (c i) t -> p c t i", i=RUN),
+            in_=hid_planes[:].rearrange("p t (c i) -> p c t i", i=RUN),
+        )
+        hid_codes = keep.tile([P, P], U32, align_bytes=64)
+        hid_scales = keep.tile([P, P], U8, align_bytes=64)
+        quantise(nc, hid_codes[:], hid_scales[:], hid_grouped[:])
+
+        regroup(nc, w2_grouped[1][:], w2_raw[1][:])
+        quantise(nc, w2_codes[:, PIECE:V], w2_scales[:, PIECE:V], w2_grouped[1][:])
+
+        half_logits = keep.tile([P, V], BF16)
+        nc.vector.tensor_scalar_mul(out=half_logits[:], in0=logits_sb[:], scalar1=0.5)
+
+        tanh_sb = keep.tile([P, V // P, P], F32)
+        out_sb = keep.tile([P, V], F32)
+        for i in range(w2_pieces):
+            for c in range(i * chunks, (i + 1) * chunks):
+                v_cols = slice(c * P, (c + 1) * P)
+                z_ps = acc_pool.tile([P, P], F32, tag="acc")
+                nc.tensor.matmul_mx(
+                    out=z_ps[:],
+                    lhsT=w2_codes[:, v_cols].bitcast(FP8X4),
+                    lhsT_scale=w2_scales[:, v_cols],
+                    rhs=hid_codes[:].bitcast(FP8X4),
+                    rhs_scale=hid_scales[:],
+                    start=True,
+                    stop=True,
+                )
+                nc.scalar.activation(
+                    out=tanh_sb[:, c, :], in_=z_ps[:], func=ACT.Tanh,
+                    bias=b2_half[:, c : c + 1], scale=0.5,
+                )
+            gate_ps = ps_pool.tile([P, chunks, P], F32, tag="gate", bufs=2)
+            for j in range(chunks):
+                nc.tensor.transpose(gate_ps[:, j, :], tanh_sb[:, i * chunks + j, :], ident_f32[:])
+            cols = slice(i * PIECE, (i + 1) * PIECE)
+            nc.vector.scalar_tensor_tensor(
+                out=out_sb[:, cols],
+                in0=gate_ps[:].rearrange("p j v -> p (j v)"),
+                scalar=3.0,
+                in1=half_logits[:, cols],
+                op0=ALU.add,
+                op1=ALU.mult,
+            )
+            nc.sync.dma_start(out=out_dram[:, cols], in_=out_sb[:, cols])

@@ -17,9 +17,10 @@ K_PASS = P * PACK
 D = 1024
 KF = 512
 V = 1024
-PIECE = 512
+W2_LOAD = 512
+W2_PIECE = 256
 RUN = 4
-VECTOR_COLS = 320
+VECTOR_SHARE = (5, 8)
 
 FLOPS = 2 * P * D * KF + 2 * P * KF * V
 
@@ -27,7 +28,7 @@ FLOPS = 2 * P * D * KF + 2 * P * KF * V
 def regroup(nc, grouped, raw):
     dst = grouped.rearrange("p (c i) j -> p c j i", i=RUN)
     src = raw.rearrange("p j (c i) -> p c j i", i=RUN)
-    cut = VECTOR_COLS // RUN
+    cut = dst.shape[1] * VECTOR_SHARE[0] // VECTOR_SHARE[1]
     nc.vector.tensor_copy(out=dst[:, :cut], in_=src[:, :cut])
     nc.scalar.copy(out=dst[:, cut:], in_=src[:, cut:])
 
@@ -48,16 +49,21 @@ def tile_sparseoutputprojection_pb_s_kernel(
     logits_dram = logits.flatten_outer_dims()
     out_dram = out.flatten_outer_dims()
     passes = D // K_PASS
-    w2_pieces = V // PIECE
-    chunks = PIECE // P
+    w2_loads = V // W2_LOAD
+    w2_pieces = V // W2_PIECE
+    pieces_per_load = W2_LOAD // W2_PIECE
+    chunks = W2_PIECE // P
 
     with ExitStack() as ctx:
         keep = ctx.enter_context(tc.tile_pool(name="keep", bufs=1))
         acc_pool = ctx.enter_context(tc.psum_pool(name="acc", bufs=4))
         ps_pool = ctx.enter_context(tc.psum_pool(name="ps", bufs=1))
+        ctx.enter_context(tc.manual_schedule())
 
+        bias_rows = keep.tile([P, P], BF16)
+        nc.vector.memset(bias_rows[:], 0.0)
         w1_raw = [keep.tile([P, PACK, KF], BF16, name="w1_raw%d" % g) for g in range(passes)]
-        w2_raw = [keep.tile([P, PACK, PIECE], BF16, name="w2_raw%d" % i) for i in range(w2_pieces)]
+        w2_raw = [keep.tile([P, PACK, W2_LOAD], BF16, name="w2_raw%d" % i) for i in range(w2_loads)]
         h_sb = keep.tile([P, D], BF16)
         logits_sb = keep.tile([P, V], BF16)
         w1_view = W_f1.rearrange("(g p j) c -> g p j c", p=P, j=PACK)
@@ -65,14 +71,11 @@ def tile_sparseoutputprojection_pb_s_kernel(
         nc.sync.dma_start(out=w1_raw[0][:], in_=w1_view[0])
         nc.sync.dma_start(out=h_sb[:], in_=h_dram)
         nc.sync.dma_start(out=w1_raw[1][:], in_=w1_view[1])
-        for i in range(w2_pieces):
-            nc.sync.dma_start(out=w2_raw[i][:], in_=w2_view[:, :, i * PIECE : (i + 1) * PIECE])
+        nc.sync.dma_start(out=bias_rows[0:4, :], in_=b_f1.rearrange("(t m) -> t m", m=P))
+        nc.sync.dma_start(out=bias_rows[4:12, :], in_=b_f2.rearrange("(c m) -> c m", m=P))
+        for i in range(w2_loads):
+            nc.sync.dma_start(out=w2_raw[i][:], in_=w2_view[:, :, i * W2_LOAD : (i + 1) * W2_LOAD])
         nc.sync.dma_start(out=logits_sb[:], in_=logits_dram)
-
-        bias_rows = keep.tile([P, P], BF16)
-        nc.vector.memset(bias_rows[:], 0.0)
-        nc.scalar.dma_start(out=bias_rows[0:4, :], in_=b_f1.rearrange("(t m) -> t m", m=P))
-        nc.scalar.dma_start(out=bias_rows[4:12, :], in_=b_f2.rearrange("(c m) -> c m", m=P))
 
         warm_in = keep.tile([P, 1], F32)
         warm_out = keep.tile([P, 1], F32)
@@ -88,16 +91,13 @@ def tile_sparseoutputprojection_pb_s_kernel(
             keep.tile([P, KF, PACK], BF16, align_bytes=64, name="w1_grouped%d" % g)
             for g in range(passes)
         ]
-        w1_codes = keep.tile([P, passes, KF], U32, align_bytes=64)
-        w1_scales = keep.tile([P, passes, KF], U8, align_bytes=64)
+        w1_codes = [
+            keep.tile([P, KF], U32, align_bytes=64, name="w1_codes%d" % g) for g in range(passes)
+        ]
+        w1_scales = [
+            keep.tile([P, KF], U8, align_bytes=64, name="w1_scales%d" % g) for g in range(passes)
+        ]
         regroup(nc, w1_grouped[0][:], w1_raw[0][:])
-
-        bias_ps = ps_pool.tile([P, P], BF16)
-        nc.tensor.transpose(bias_ps[:], bias_rows[:], ident_bf16[:])
-        b1_col = keep.tile([P, 4], F32)
-        b2_half = keep.tile([P, 8], F32)
-        nc.vector.tensor_copy(out=b1_col[:], in_=bias_ps[:, 0:4])
-        nc.vector.tensor_scalar_mul(out=b2_half[:], in0=bias_ps[:, 4:12], scalar1=0.5)
 
         h_words = h_sb[:].bitcast(F32).rearrange("r (g q u) -> r g u q", g=passes, u=2)
         hT_ps = ps_pool.tile([P, passes, 2, P], F32)
@@ -112,15 +112,21 @@ def tile_sparseoutputprojection_pb_s_kernel(
         h_codes = keep.tile([P, passes, P], U32, align_bytes=64)
         h_scales = keep.tile([P, passes, P], U8, align_bytes=64)
 
-        quantise(nc, w1_codes[:, 0, :], w1_scales[:, 0, :], w1_grouped[0][:])
+        quantise(nc, w1_codes[0][:], w1_scales[0][:], w1_grouped[0][:])
+        regroup(nc, w1_grouped[1][:], w1_raw[1][:])
         nc.vector.quantize_mx(
             out=h_codes[:].rearrange("p g r -> p (g r)").bitcast(FP8X4),
             scales=h_scales[:].rearrange("p g r -> p (g r)"),
             in_=h_grouped[:],
         )
+        quantise(nc, w1_codes[1][:], w1_scales[1][:], w1_grouped[1][:])
 
-        regroup(nc, w1_grouped[1][:], w1_raw[1][:])
-        quantise(nc, w1_codes[:, 1, :], w1_scales[:, 1, :], w1_grouped[1][:])
+        bias_ps = ps_pool.tile([P, P], BF16)
+        nc.tensor.transpose(bias_ps[:], bias_rows[:], ident_bf16[:])
+        b1_col = keep.tile([P, 4], F32)
+        b2_half = keep.tile([P, 8], F32)
+        nc.vector.tensor_copy(out=b1_col[:], in_=bias_ps[:, 0:4])
+        nc.vector.tensor_scalar_mul(out=b2_half[:], in0=bias_ps[:, 4:12], scalar1=0.5)
 
         hid_ps = [acc_pool.tile([P, P], F32, tag="acc", name="hid_ps%d" % t) for t in range(PACK)]
         for g in range(passes):
@@ -128,8 +134,8 @@ def tile_sparseoutputprojection_pb_s_kernel(
                 m_cols = slice(t * P, (t + 1) * P)
                 nc.tensor.matmul_mx(
                     out=hid_ps[t][:],
-                    lhsT=w1_codes[:, g, m_cols].bitcast(FP8X4),
-                    lhsT_scale=w1_scales[:, g, m_cols],
+                    lhsT=w1_codes[g][:, m_cols].bitcast(FP8X4),
+                    lhsT_scale=w1_scales[g][:, m_cols],
                     rhs=h_codes[:, g, :].bitcast(FP8X4),
                     rhs_scale=h_scales[:, g, :],
                     start=(g == 0),
@@ -137,13 +143,29 @@ def tile_sparseoutputprojection_pb_s_kernel(
                 )
 
         w2_grouped = [
-            keep.tile([P, PIECE, PACK], BF16, align_bytes=64, name="w2_grouped%d" % i)
+            keep.tile([P, W2_PIECE, PACK], BF16, align_bytes=64, name="w2_grouped%d" % i)
             for i in range(w2_pieces)
         ]
-        w2_codes = keep.tile([P, V], U32, align_bytes=64)
-        w2_scales = keep.tile([P, V], U8, align_bytes=64)
-        regroup(nc, w2_grouped[0][:], w2_raw[0][:])
-        quantise(nc, w2_codes[:, 0:PIECE], w2_scales[:, 0:PIECE], w2_grouped[0][:])
+        w2_codes = [
+            keep.tile([P, W2_PIECE], U32, align_bytes=64, name="w2_codes%d" % i)
+            for i in range(w2_pieces)
+        ]
+        w2_scales = [
+            keep.tile([P, W2_PIECE], U8, align_bytes=64, name="w2_scales%d" % i)
+            for i in range(w2_pieces)
+        ]
+
+        def regroup_w2(i):
+            first = (i % pieces_per_load) * W2_PIECE
+            regroup(nc, w2_grouped[i][:], w2_raw[i // pieces_per_load][:, :, first : first + W2_PIECE])
+
+        def quantise_w2(i):
+            quantise(nc, w2_codes[i][:], w2_scales[i][:], w2_grouped[i][:])
+
+        for i in range(pieces_per_load):
+            regroup_w2(i)
+        for i in range(pieces_per_load):
+            quantise_w2(i)
 
         hid_planes = keep.tile([P, PACK, P], BF16)
         for t in range(PACK):
@@ -160,41 +182,52 @@ def tile_sparseoutputprojection_pb_s_kernel(
         hid_scales = keep.tile([P, P], U8, align_bytes=64)
         quantise(nc, hid_codes[:], hid_scales[:], hid_grouped[:])
 
-        regroup(nc, w2_grouped[1][:], w2_raw[1][:])
-        quantise(nc, w2_codes[:, PIECE:V], w2_scales[:, PIECE:V], w2_grouped[1][:])
+        for i in range(pieces_per_load, w2_pieces):
+            regroup_w2(i)
+            quantise_w2(i)
 
         half_logits = keep.tile([P, V], BF16)
         nc.vector.tensor_scalar_mul(out=half_logits[:], in0=logits_sb[:], scalar1=0.5)
 
-        tanh_sb = keep.tile([P, V // P, P], F32)
-        out_sb = keep.tile([P, V], F32)
-        for i in range(w2_pieces):
-            for c in range(i * chunks, (i + 1) * chunks):
-                v_cols = slice(c * P, (c + 1) * P)
+        tanh_sb = [keep.tile([P, chunks, P], F32, name="tanh_sb%d" % i) for i in range(w2_pieces)]
+
+        def product(i):
+            for j in range(chunks):
+                c = i * chunks + j
+                v_cols = slice(j * P, (j + 1) * P)
                 z_ps = acc_pool.tile([P, P], F32, tag="acc")
                 nc.tensor.matmul_mx(
                     out=z_ps[:],
-                    lhsT=w2_codes[:, v_cols].bitcast(FP8X4),
-                    lhsT_scale=w2_scales[:, v_cols],
+                    lhsT=w2_codes[i][:, v_cols].bitcast(FP8X4),
+                    lhsT_scale=w2_scales[i][:, v_cols],
                     rhs=hid_codes[:].bitcast(FP8X4),
                     rhs_scale=hid_scales[:],
                     start=True,
                     stop=True,
                 )
                 nc.scalar.activation(
-                    out=tanh_sb[:, c, :], in_=z_ps[:], func=ACT.Tanh,
+                    out=tanh_sb[i][:, j, :], in_=z_ps[:], func=ACT.Tanh,
                     bias=b2_half[:, c : c + 1], scale=0.5,
                 )
+
+        def finish(i):
             gate_ps = ps_pool.tile([P, chunks, P], F32, tag="gate", bufs=2)
             for j in range(chunks):
-                nc.tensor.transpose(gate_ps[:, j, :], tanh_sb[:, i * chunks + j, :], ident_f32[:])
-            cols = slice(i * PIECE, (i + 1) * PIECE)
+                nc.tensor.transpose(gate_ps[:, j, :], tanh_sb[i][:, j, :], ident_f32[:])
+            cols = slice(i * W2_PIECE, (i + 1) * W2_PIECE)
+            out_sb = keep.tile([P, W2_PIECE], F32, name="out_sb%d" % i)
             nc.vector.scalar_tensor_tensor(
-                out=out_sb[:, cols],
+                out=out_sb[:],
                 in0=gate_ps[:].rearrange("p j v -> p (j v)"),
                 scalar=3.0,
                 in1=half_logits[:, cols],
                 op0=ALU.add,
                 op1=ALU.mult,
             )
-            nc.sync.dma_start(out=out_dram[:, cols], in_=out_sb[:, cols])
+            nc.sync.dma_start(out=out_dram[:, cols], in_=out_sb[:])
+
+        product(0)
+        for i in range(1, w2_pieces):
+            product(i)
+            finish(i - 1)
+        finish(w2_pieces - 1)

@@ -226,8 +226,7 @@ def tile_sparseoutputprojection_pb_s_kernel(
             )
             nc.sync.dma_start(out=out_dram[:, cols], in_=out_sb[:])
 
-        product(0)
-        for i in range(1, w2_pieces):
+        for i in range(w2_pieces):
             product(i)
-            finish(i - 1)
-        finish(w2_pieces - 1)
+        for i in range(w2_pieces):
+            finish(i)

@@ -20,15 +20,18 @@ V = 1024
 W2_LOAD = 512
 W2_PIECE = 256
 RUN = 4
-VECTOR_SHARE = (5, 8)
+W1_VECTOR_SHARE = (3, 4)
+W2_VECTOR_SHARE = (1, 2)
+FINISH_LAG = 1
+WARM_PASSES = 3
 
 FLOPS = 2 * P * D * KF + 2 * P * KF * V
 
 
-def regroup(nc, grouped, raw):
+def regroup(nc, grouped, raw, vector_share):
     dst = grouped.rearrange("p (c i) j -> p c j i", i=RUN)
     src = raw.rearrange("p j (c i) -> p c j i", i=RUN)
-    cut = dst.shape[1] * VECTOR_SHARE[0] // VECTOR_SHARE[1]
+    cut = dst.shape[1] * vector_share[0] // vector_share[1]
     nc.vector.tensor_copy(out=dst[:, :cut], in_=src[:, :cut])
     nc.scalar.copy(out=dst[:, cut:], in_=src[:, cut:])
 
@@ -97,7 +100,7 @@ def tile_sparseoutputprojection_pb_s_kernel(
         w1_scales = [
             keep.tile([P, KF], U8, align_bytes=64, name="w1_scales%d" % g) for g in range(passes)
         ]
-        regroup(nc, w1_grouped[0][:], w1_raw[0][:])
+        regroup(nc, w1_grouped[0][:], w1_raw[0][:], W1_VECTOR_SHARE)
 
         h_words = h_sb[:].bitcast(F32).rearrange("r (g q u) -> r g u q", g=passes, u=2)
         hT_ps = ps_pool.tile([P, passes, 2, P], F32)
@@ -113,7 +116,7 @@ def tile_sparseoutputprojection_pb_s_kernel(
         h_scales = keep.tile([P, passes, P], U8, align_bytes=64)
 
         quantise(nc, w1_codes[0][:], w1_scales[0][:], w1_grouped[0][:])
-        regroup(nc, w1_grouped[1][:], w1_raw[1][:])
+        regroup(nc, w1_grouped[1][:], w1_raw[1][:], W1_VECTOR_SHARE)
         nc.vector.quantize_mx(
             out=h_codes[:].rearrange("p g r -> p (g r)").bitcast(FP8X4),
             scales=h_scales[:].rearrange("p g r -> p (g r)"),
@@ -142,6 +145,18 @@ def tile_sparseoutputprojection_pb_s_kernel(
                     stop=(g == passes - 1),
                 )
 
+        warm_ps = ps_pool.tile([P, KF], F32, tag="hT_ps")
+        for n in range(WARM_PASSES):
+            nc.tensor.matmul_mx(
+                out=warm_ps[:],
+                lhsT=w1_codes[0][:, 0:P].bitcast(FP8X4),
+                lhsT_scale=w1_scales[0][:, 0:P],
+                rhs=w1_codes[0][:].bitcast(FP8X4),
+                rhs_scale=w1_scales[0][:],
+                start=(n == 0),
+                stop=(n == WARM_PASSES - 1),
+            )
+
         w2_grouped = [
             keep.tile([P, W2_PIECE, PACK], BF16, align_bytes=64, name="w2_grouped%d" % i)
             for i in range(w2_pieces)
@@ -157,15 +172,15 @@ def tile_sparseoutputprojection_pb_s_kernel(
 
         def regroup_w2(i):
             first = (i % pieces_per_load) * W2_PIECE
-            regroup(nc, w2_grouped[i][:], w2_raw[i // pieces_per_load][:, :, first : first + W2_PIECE])
+            raw = w2_raw[i // pieces_per_load][:, :, first : first + W2_PIECE]
+            regroup(nc, w2_grouped[i][:], raw, W2_VECTOR_SHARE)
 
         def quantise_w2(i):
             quantise(nc, w2_codes[i][:], w2_scales[i][:], w2_grouped[i][:])
 
         for i in range(pieces_per_load):
             regroup_w2(i)
-        for i in range(pieces_per_load):
-            quantise_w2(i)
+        quantise_w2(0)
 
         hid_planes = keep.tile([P, PACK, P], BF16)
         for t in range(PACK):
@@ -173,6 +188,8 @@ def tile_sparseoutputprojection_pb_s_kernel(
                 out=hid_planes[:, t, :], in_=hid_ps[t][:], func=ACT.Gelu,
                 bias=b1_col[:, t : t + 1], scale=1.0,
             )
+        for i in range(pieces_per_load, w2_pieces):
+            regroup_w2(i)
         hid_grouped = keep.tile([P, P, PACK], BF16, align_bytes=64)
         nc.vector.tensor_copy(
             out=hid_grouped[:].rearrange("p (c i) t -> p c t i", i=RUN),
@@ -182,8 +199,7 @@ def tile_sparseoutputprojection_pb_s_kernel(
         hid_scales = keep.tile([P, P], U8, align_bytes=64)
         quantise(nc, hid_codes[:], hid_scales[:], hid_grouped[:])
 
-        for i in range(pieces_per_load, w2_pieces):
-            regroup_w2(i)
+        for i in range(1, w2_pieces):
             quantise_w2(i)
 
         half_logits = keep.tile([P, V], BF16)
@@ -226,7 +242,8 @@ def tile_sparseoutputprojection_pb_s_kernel(
             )
             nc.sync.dma_start(out=out_dram[:, cols], in_=out_sb[:])
 
-        for i in range(w2_pieces):
-            product(i)
-        for i in range(w2_pieces):
-            finish(i)
+        for i in range(w2_pieces + FINISH_LAG):
+            if i < w2_pieces:
+                product(i)
+            if i >= FINISH_LAG:
+                finish(i - FINISH_LAG)

@@ -22,7 +22,7 @@ W2_PIECE = 256
 RUN = 4
 W1_VECTOR_SHARE = (3, 4)
 W2_VECTOR_SHARE = (1, 2)
-FINISH_LAG = 1
+FINISH_LAG = 2
 WARM_PASSES = 3
 
 FLOPS = 2 * P * D * KF + 2 * P * KF * V
@@ -124,7 +124,7 @@ def tile_sparseoutputprojection_pb_s_kernel(
         )
         quantise(nc, w1_codes[1][:], w1_scales[1][:], w1_grouped[1][:])
 
-        bias_ps = ps_pool.tile([P, P], BF16)
+        bias_ps = ps_pool.tile([P, P], BF16, tag="hT_ps")
         nc.tensor.transpose(bias_ps[:], bias_rows[:], ident_bf16[:])
         b1_col = keep.tile([P, 4], F32)
         b2_half = keep.tile([P, 8], F32)
@@ -208,12 +208,11 @@ def tile_sparseoutputprojection_pb_s_kernel(
         tanh_sb = [keep.tile([P, chunks, P], F32, name="tanh_sb%d" % i) for i in range(w2_pieces)]
 
         def product(i):
+            z_ps = acc_pool.tile([P, chunks, P], F32, tag="acc")
             for j in range(chunks):
-                c = i * chunks + j
                 v_cols = slice(j * P, (j + 1) * P)
-                z_ps = acc_pool.tile([P, P], F32, tag="acc")
                 nc.tensor.matmul_mx(
-                    out=z_ps[:],
+                    out=z_ps[:, j, :],
                     lhsT=w2_codes[i][:, v_cols].bitcast(FP8X4),
                     lhsT_scale=w2_scales[i][:, v_cols],
                     rhs=hid_codes[:].bitcast(FP8X4),
@@ -221,26 +220,33 @@ def tile_sparseoutputprojection_pb_s_kernel(
                     start=True,
                     stop=True,
                 )
+            for j in range(chunks):
+                c = i * chunks + j
                 nc.scalar.activation(
-                    out=tanh_sb[i][:, j, :], in_=z_ps[:], func=ACT.Tanh,
+                    out=tanh_sb[i][:, j, :], in_=z_ps[:, j, :], func=ACT.Tanh,
                     bias=b2_half[:, c : c + 1], scale=0.5,
                 )
 
         def finish(i):
-            gate_ps = ps_pool.tile([P, chunks, P], F32, tag="gate", bufs=2)
-            for j in range(chunks):
-                nc.tensor.transpose(gate_ps[:, j, :], tanh_sb[i][:, j, :], ident_f32[:])
-            cols = slice(i * W2_PIECE, (i + 1) * W2_PIECE)
-            out_sb = keep.tile([P, W2_PIECE], F32, name="out_sb%d" % i)
-            nc.vector.scalar_tensor_tensor(
-                out=out_sb[:],
-                in0=gate_ps[:].rearrange("p j v -> p (j v)"),
-                scalar=3.0,
-                in1=half_logits[:, cols],
-                op0=ALU.add,
-                op1=ALU.mult,
-            )
-            nc.sync.dma_start(out=out_dram[:, cols], in_=out_sb[:])
+            step = 1 if i == w2_pieces - 1 else chunks
+            for first in range(0, chunks, step):
+                gate_ps = ps_pool.tile([P, chunks, P], F32, tag="gate", bufs=3)
+                for j in range(step):
+                    nc.tensor.transpose(
+                        gate_ps[:, j, :], tanh_sb[i][:, first + j, :], ident_f32[:]
+                    )
+                start = i * W2_PIECE + first * P
+                cols = slice(start, start + step * P)
+                out_sb = keep.tile([P, step * P], F32, name="out_sb%d_%d" % (i, first))
+                nc.vector.scalar_tensor_tensor(
+                    out=out_sb[:],
+                    in0=gate_ps[:, 0:step, :].rearrange("p j v -> p (j v)"),
+                    scalar=3.0,
+                    in1=half_logits[:, cols],
+                    op0=ALU.add,
+                    op1=ALU.mult,
+                )
+                nc.sync.dma_start(out=out_dram[:, cols], in_=out_sb[:])
 
         for i in range(w2_pieces + FINISH_LAG):
             if i < w2_pieces:

@@ -20,10 +20,11 @@ V = 1024
 W2_LOAD = 512
 W2_PIECE = 256
 RUN = 4
-W1_VECTOR_SHARE = (3, 4)
-W2_VECTOR_SHARE = (1, 2)
+W1_VECTOR_SHARE = (((1, 1), (0, 1)), ((1, 1), (1, 2)))
+W2_VECTOR_SHARE = ((1, 2), (1, 2), (1, 2), (1, 4))
 FINISH_LAG = 2
-WARM_PASSES = 3
+EARLY_WARM_PASSES = 4
+WARM_PASSES = 6
 
 FLOPS = 2 * P * D * KF + 2 * P * KF * V
 
@@ -32,8 +33,10 @@ def regroup(nc, grouped, raw, vector_share):
     dst = grouped.rearrange("p (c i) j -> p c j i", i=RUN)
     src = raw.rearrange("p j (c i) -> p c j i", i=RUN)
     cut = dst.shape[1] * vector_share[0] // vector_share[1]
-    nc.vector.tensor_copy(out=dst[:, :cut], in_=src[:, :cut])
-    nc.scalar.copy(out=dst[:, cut:], in_=src[:, cut:])
+    if cut > 0:
+        nc.vector.tensor_copy(out=dst[:, :cut], in_=src[:, :cut])
+    if cut < dst.shape[1]:
+        nc.scalar.copy(out=dst[:, cut:], in_=src[:, cut:])
 
 
 def quantise(nc, codes, scales, grouped):
@@ -64,7 +67,7 @@ def tile_sparseoutputprojection_pb_s_kernel(
         ctx.enter_context(tc.manual_schedule())
 
         bias_rows = keep.tile([P, P], BF16)
-        nc.vector.memset(bias_rows[:], 0.0)
+        nc.gpsimd.memset(bias_rows[:], 0.0)
         w1_raw = [keep.tile([P, PACK, KF], BF16, name="w1_raw%d" % g) for g in range(passes)]
         w2_raw = [keep.tile([P, PACK, W2_LOAD], BF16, name="w2_raw%d" % i) for i in range(w2_loads)]
         h_sb = keep.tile([P, D], BF16)
@@ -72,10 +75,10 @@ def tile_sparseoutputprojection_pb_s_kernel(
         w1_view = W_f1.rearrange("(g p j) c -> g p j c", p=P, j=PACK)
         w2_view = W_f2.rearrange("(t p) n -> p t n", p=P)
         nc.sync.dma_start(out=w1_raw[0][:], in_=w1_view[0])
-        nc.sync.dma_start(out=h_sb[:], in_=h_dram)
-        nc.sync.dma_start(out=w1_raw[1][:], in_=w1_view[1])
         nc.sync.dma_start(out=bias_rows[0:4, :], in_=b_f1.rearrange("(t m) -> t m", m=P))
         nc.sync.dma_start(out=bias_rows[4:12, :], in_=b_f2.rearrange("(c m) -> c m", m=P))
+        nc.sync.dma_start(out=h_sb[:], in_=h_dram)
+        nc.sync.dma_start(out=w1_raw[1][:], in_=w1_view[1])
         for i in range(w2_loads):
             nc.sync.dma_start(out=w2_raw[i][:], in_=w2_view[:, :, i * W2_LOAD : (i + 1) * W2_LOAD])
         nc.sync.dma_start(out=logits_sb[:], in_=logits_dram)
@@ -100,7 +103,38 @@ def tile_sparseoutputprojection_pb_s_kernel(
         w1_scales = [
             keep.tile([P, KF], U8, align_bytes=64, name="w1_scales%d" % g) for g in range(passes)
         ]
-        regroup(nc, w1_grouped[0][:], w1_raw[0][:], W1_VECTOR_SHARE)
+        halves = [slice(i * KF // 2, (i + 1) * KF // 2) for i in range(2)]
+
+        def regroup_w1(g, i):
+            cols = halves[i]
+            share = W1_VECTOR_SHARE[g][i]
+            regroup(nc, w1_grouped[g][:, cols, :], w1_raw[g][:, :, cols], share)
+
+        def quantise_w1(g, i):
+            cols = halves[i]
+            quantise(nc, w1_codes[g][:, cols], w1_scales[g][:, cols], w1_grouped[g][:, cols, :])
+
+        def warm(warm_ps, warm_passes, width):
+            for n in range(warm_passes):
+                nc.tensor.matmul_mx(
+                    out=warm_ps[:, 0:width],
+                    lhsT=w1_codes[0][:, 0:P].bitcast(FP8X4),
+                    lhsT_scale=w1_scales[0][:, 0:P],
+                    rhs=w1_codes[0][:, 0:width].bitcast(FP8X4),
+                    rhs_scale=w1_scales[0][:, 0:width],
+                    start=(n == 0),
+                    stop=(n == warm_passes - 1),
+                )
+
+        regroup_w1(0, 0)
+        regroup_w1(0, 1)
+
+        bias_ps = acc_pool.tile([P, P], BF16, tag="acc")
+        nc.tensor.transpose(bias_ps[:], bias_rows[:], ident_bf16[:])
+        b1_col = keep.tile([P, 4], F32)
+        b2_half = keep.tile([P, 8], F32)
+        nc.vector.tensor_copy(out=b1_col[:], in_=bias_ps[:, 0:4])
+        nc.vector.tensor_scalar_mul(out=b2_half[:], in0=bias_ps[:, 4:12], scalar1=0.5)
 
         h_words = h_sb[:].bitcast(F32).rearrange("r (g q u) -> r g u q", g=passes, u=2)
         hT_ps = ps_pool.tile([P, passes, 2, P], F32)
@@ -115,21 +149,19 @@ def tile_sparseoutputprojection_pb_s_kernel(
         h_codes = keep.tile([P, passes, P], U32, align_bytes=64)
         h_scales = keep.tile([P, passes, P], U8, align_bytes=64)
 
-        quantise(nc, w1_codes[0][:], w1_scales[0][:], w1_grouped[0][:])
-        regroup(nc, w1_grouped[1][:], w1_raw[1][:], W1_VECTOR_SHARE)
+        quantise_w1(0, 0)
+        early_warm_ps = ps_pool.tile([P, KF], F32, tag="gate", bufs=3)
+        warm(early_warm_ps, EARLY_WARM_PASSES, KF // 2)
+        quantise_w1(0, 1)
+        regroup_w1(1, 0)
+        regroup_w1(1, 1)
         nc.vector.quantize_mx(
             out=h_codes[:].rearrange("p g r -> p (g r)").bitcast(FP8X4),
             scales=h_scales[:].rearrange("p g r -> p (g r)"),
             in_=h_grouped[:],
         )
-        quantise(nc, w1_codes[1][:], w1_scales[1][:], w1_grouped[1][:])
-
-        bias_ps = ps_pool.tile([P, P], BF16, tag="hT_ps")
-        nc.tensor.transpose(bias_ps[:], bias_rows[:], ident_bf16[:])
-        b1_col = keep.tile([P, 4], F32)
-        b2_half = keep.tile([P, 8], F32)
-        nc.vector.tensor_copy(out=b1_col[:], in_=bias_ps[:, 0:4])
-        nc.vector.tensor_scalar_mul(out=b2_half[:], in0=bias_ps[:, 4:12], scalar1=0.5)
+        quantise_w1(1, 0)
+        quantise_w1(1, 1)
 
         hid_ps = [acc_pool.tile([P, P], F32, tag="acc", name="hid_ps%d" % t) for t in range(PACK)]
         for g in range(passes):
@@ -145,17 +177,8 @@ def tile_sparseoutputprojection_pb_s_kernel(
                     stop=(g == passes - 1),
                 )
 
-        warm_ps = ps_pool.tile([P, KF], F32, tag="hT_ps")
-        for n in range(WARM_PASSES):
-            nc.tensor.matmul_mx(
-                out=warm_ps[:],
-                lhsT=w1_codes[0][:, 0:P].bitcast(FP8X4),
-                lhsT_scale=w1_scales[0][:, 0:P],
-                rhs=w1_codes[0][:].bitcast(FP8X4),
-                rhs_scale=w1_scales[0][:],
-                start=(n == 0),
-                stop=(n == WARM_PASSES - 1),
-            )
+        late_warm_ps = ps_pool.tile([P, KF], F32, tag="hT_ps")
+        warm(late_warm_ps, WARM_PASSES, KF)
 
         w2_grouped = [
             keep.tile([P, W2_PIECE, PACK], BF16, align_bytes=64, name="w2_grouped%d" % i)
@@ -173,7 +196,7 @@ def tile_sparseoutputprojection_pb_s_kernel(
         def regroup_w2(i):
             first = (i % pieces_per_load) * W2_PIECE
             raw = w2_raw[i // pieces_per_load][:, :, first : first + W2_PIECE]
-            regroup(nc, w2_grouped[i][:], raw, W2_VECTOR_SHARE)
+            regroup(nc, w2_grouped[i][:], raw, W2_VECTOR_SHARE[i])
 
         def quantise_w2(i):
             quantise(nc, w2_codes[i][:], w2_scales[i][:], w2_grouped[i][:])
@@ -188,8 +211,7 @@ def tile_sparseoutputprojection_pb_s_kernel(
                 out=hid_planes[:, t, :], in_=hid_ps[t][:], func=ACT.Gelu,
                 bias=b1_col[:, t : t + 1], scale=1.0,
             )
-        for i in range(pieces_per_load, w2_pieces):
-            regroup_w2(i)
+        regroup_w2(2)
         hid_grouped = keep.tile([P, P, PACK], BF16, align_bytes=64)
         nc.vector.tensor_copy(
             out=hid_grouped[:].rearrange("p (c i) t -> p c t i", i=RUN),
@@ -199,8 +221,10 @@ def tile_sparseoutputprojection_pb_s_kernel(
         hid_scales = keep.tile([P, P], U8, align_bytes=64)
         quantise(nc, hid_codes[:], hid_scales[:], hid_grouped[:])
 
-        for i in range(1, w2_pieces):
-            quantise_w2(i)
+        quantise_w2(1)
+        regroup_w2(3)
+        quantise_w2(2)
+        quantise_w2(3)
 
         half_logits = keep.tile([P, V], BF16)
         nc.vector.tensor_scalar_mul(out=half_logits[:], in0=logits_sb[:], scalar1=0.5)
@@ -230,7 +254,10 @@ def tile_sparseoutputprojection_pb_s_kernel(
         def finish(i):
             step = 1 if i == w2_pieces - 1 else chunks
             for first in range(0, chunks, step):
-                gate_ps = ps_pool.tile([P, chunks, P], F32, tag="gate", bufs=3)
+                if first > 0:
+                    gate_ps = ps_pool.tile([P, chunks, P], F32, tag="hT_ps")
+                else:
+                    gate_ps = ps_pool.tile([P, chunks, P], F32, tag="gate", bufs=3)
                 for j in range(step):
                     nc.tensor.transpose(
                         gate_ps[:, j, :], tanh_sb[i][:, first + j, :], ident_f32[:]

@@ -20,8 +20,8 @@ V = 1024
 W2_LOAD = 512
 W2_PIECE = 256
 RUN = 4
-W1_VECTOR_SHARE = (((1, 1), (0, 1)), ((1, 1), (1, 2)))
-W2_VECTOR_SHARE = ((1, 2), (1, 2), (1, 2), (1, 4))
+W1_VECTOR_SHARE = (((1, 1), (0, 1)), ((1, 1), (1, 4)))
+W2_VECTOR_SHARE = ((5, 8), (5, 8), (1, 2), (1, 4))
 FINISH_LAG = 2
 EARLY_WARM_PASSES = 4
 WARM_PASSES = 6
@@ -137,15 +137,18 @@ def tile_sparseoutputprojection_pb_s_kernel(
         nc.vector.tensor_scalar_mul(out=b2_half[:], in0=bias_ps[:, 4:12], scalar1=0.5)
 
         h_words = h_sb[:].bitcast(F32).rearrange("r (g q u) -> r g u q", g=passes, u=2)
-        hT_ps = ps_pool.tile([P, passes, 2, P], F32)
-        for g in range(passes):
-            for u in range(2):
-                nc.tensor.transpose(hT_ps[:, g, u, :], h_words[:, g, u, :], ident_f32[:])
         h_grouped = keep.tile([P, passes * P * PACK], BF16, align_bytes=64)
-        nc.scalar.copy(
-            out=h_grouped[:].bitcast(F32).rearrange("p (g r u) -> p g r u", g=passes, u=2),
-            in_=hT_ps[:].rearrange("p g u r -> p g r u"),
-        )
+        h_grouped_words = h_grouped[:].bitcast(F32).rearrange("p (g r u) -> p g r u", g=passes, u=2)
+        for g in range(passes):
+            if g == 0:
+                hT_ps = ps_pool.tile([P, 2, P], F32, tag="hT_ps")
+            else:
+                hT_ps = ps_pool.tile([P, 2, P], F32, tag="gate", bufs=3)
+            for u in range(2):
+                nc.tensor.transpose(hT_ps[:, u, :], h_words[:, g, u, :], ident_f32[:])
+            nc.scalar.copy(
+                out=h_grouped_words[:, g, :, :], in_=hT_ps[:].rearrange("p u r -> p r u")
+            )
         h_codes = keep.tile([P, passes, P], U32, align_bytes=64)
         h_scales = keep.tile([P, passes, P], U8, align_bytes=64)
 
@@ -217,12 +220,12 @@ def tile_sparseoutputprojection_pb_s_kernel(
             out=hid_grouped[:].rearrange("p (c i) t -> p c t i", i=RUN),
             in_=hid_planes[:].rearrange("p t (c i) -> p c t i", i=RUN),
         )
+        regroup_w2(3)
         hid_codes = keep.tile([P, P], U32, align_bytes=64)
         hid_scales = keep.tile([P, P], U8, align_bytes=64)
         quantise(nc, hid_codes[:], hid_scales[:], hid_grouped[:])
 
         quantise_w2(1)
-        regroup_w2(3)
         quantise_w2(2)
         quantise_w2(3)
 

@@ -23,7 +23,8 @@ RUN = 4
 W1_VECTOR_SHARE = (((1, 1), (0, 1)), ((1, 1), (1, 4)))
 W2_VECTOR_SHARE = ((5, 8), (5, 8), (1, 2), (1, 4))
 FINISH_LAG = 2
-EARLY_WARM_PASSES = 4
+FIRST_WARM_PASSES = 5
+EARLY_WARM_PASSES = 6
 WARM_PASSES = 6
 
 FLOPS = 2 * P * D * KF + 2 * P * KF * V
@@ -83,6 +84,8 @@ def tile_sparseoutputprojection_pb_s_kernel(
             nc.sync.dma_start(out=w2_raw[i][:], in_=w2_view[:, :, i * W2_LOAD : (i + 1) * W2_LOAD])
         nc.sync.dma_start(out=logits_sb[:], in_=logits_dram)
 
+        zeros_f32 = keep.tile([P, P], F32)
+        nc.vector.memset(zeros_f32[:], 0.0)
         warm_in = keep.tile([P, 1], F32)
         warm_out = keep.tile([P, 1], F32)
         nc.vector.memset(warm_in[:], 0.0)
@@ -129,6 +132,12 @@ def tile_sparseoutputprojection_pb_s_kernel(
         regroup_w1(0, 0)
         regroup_w1(0, 1)
 
+        first_warm_ps = ps_pool.tile([P, P], F32, tag="gate", bufs=3)
+        for n in range(FIRST_WARM_PASSES):
+            nc.tensor.matmul(
+                out=first_warm_ps[:], lhsT=zeros_f32[:], rhs=zeros_f32[:],
+                start=(n == 0), stop=(n == FIRST_WARM_PASSES - 1),
+            )
         bias_ps = acc_pool.tile([P, P], BF16, tag="acc")
         nc.tensor.transpose(bias_ps[:], bias_rows[:], ident_bf16[:])
         b1_col = keep.tile([P, 4], F32)

@@ -264,28 +264,23 @@ def tile_sparseoutputprojection_pb_s_kernel(
                 )
 
         def finish(i):
-            step = 1 if i == w2_pieces - 1 else chunks
-            for first in range(0, chunks, step):
-                if first > 0:
-                    gate_ps = ps_pool.tile([P, chunks, P], F32, tag="hT_ps")
-                else:
-                    gate_ps = ps_pool.tile([P, chunks, P], F32, tag="gate", bufs=3)
-                for j in range(step):
-                    nc.tensor.transpose(
-                        gate_ps[:, j, :], tanh_sb[i][:, first + j, :], ident_f32[:]
-                    )
-                start = i * W2_PIECE + first * P
-                cols = slice(start, start + step * P)
-                out_sb = keep.tile([P, step * P], F32, name="out_sb%d_%d" % (i, first))
-                nc.vector.scalar_tensor_tensor(
-                    out=out_sb[:],
-                    in0=gate_ps[:, 0:step, :].rearrange("p j v -> p (j v)"),
-                    scalar=3.0,
-                    in1=half_logits[:, cols],
-                    op0=ALU.add,
-                    op1=ALU.mult,
-                )
-                nc.sync.dma_start(out=out_dram[:, cols], in_=out_sb[:])
+            if i == w2_pieces - 1:
+                gate_ps = ps_pool.tile([P, chunks, P], F32, tag="hT_ps")
+            else:
+                gate_ps = ps_pool.tile([P, chunks, P], F32, tag="gate", bufs=3)
+            for j in range(chunks):
+                nc.tensor.transpose(gate_ps[:, j, :], tanh_sb[i][:, j, :], ident_f32[:])
+            cols = slice(i * W2_PIECE, (i + 1) * W2_PIECE)
+            out_sb = keep.tile([P, W2_PIECE], F32, name="out_sb%d" % i)
+            nc.vector.scalar_tensor_tensor(
+                out=out_sb[:],
+                in0=gate_ps[:].rearrange("p j v -> p (j v)"),
+                scalar=3.0,
+                in1=half_logits[:, cols],
+                op0=ALU.add,
+                op1=ALU.mult,
+            )
+            nc.sync.dma_start(out=out_dram[:, cols], in_=out_sb[:])
 
         for i in range(w2_pieces + FINISH_LAG):
             if i < w2_pieces:

from contextlib import ExitStack

import concourse.mybir as mybir
from concourse.masks import make_identity

BF16 = mybir.dt.bfloat16
F32 = mybir.dt.float32
U32 = mybir.dt.uint32
U8 = mybir.dt.uint8
FP8X4 = mybir.dt.float8_e4m3fn_x4
ACT = mybir.ActivationFunctionType
ALU = mybir.AluOpType

P = 128
PACK = 4
K_PASS = P * PACK
D = 1024
KF = 512
V = 1024
W2_LOAD = 512
W2_PIECE = 256
RUN = 4
W1_VECTOR_SHARE = (((1, 1), (0, 1)), ((1, 1), (1, 4)))
W2_VECTOR_SHARE = ((5, 8), (5, 8), (1, 2), (1, 4))
FINISH_LAG = 2
FIRST_WARM_PASSES = 5
EARLY_WARM_PASSES = 6
WARM_PASSES = 6

FLOPS = 2 * P * D * KF + 2 * P * KF * V


def regroup(nc, grouped, raw, vector_share):
    dst = grouped.rearrange("p (c i) j -> p c j i", i=RUN)
    src = raw.rearrange("p j (c i) -> p c j i", i=RUN)
    cut = dst.shape[1] * vector_share[0] // vector_share[1]
    if cut > 0:
        nc.vector.tensor_copy(out=dst[:, :cut], in_=src[:, :cut])
    if cut < dst.shape[1]:
        nc.scalar.copy(out=dst[:, cut:], in_=src[:, cut:])


def quantise(nc, codes, scales, grouped):
    nc.vector.quantize_mx(
        out=codes.bitcast(FP8X4),
        scales=scales,
        in_=grouped.rearrange("p w j -> p (w j)"),
    )


def tile_sparseoutputprojection_pb_s_kernel(
    tc, hidden_states, logits, W_f1, b_f1, W_f2, b_f2, out
):
    nc = tc.nc
    h_dram = hidden_states.flatten_outer_dims()
    logits_dram = logits.flatten_outer_dims()
    out_dram = out.flatten_outer_dims()
    passes = D // K_PASS
    w2_loads = V // W2_LOAD
    w2_pieces = V // W2_PIECE
    pieces_per_load = W2_LOAD // W2_PIECE
    chunks = W2_PIECE // P

    with ExitStack() as ctx:
        keep = ctx.enter_context(tc.tile_pool(name="keep", bufs=1))
        acc_pool = ctx.enter_context(tc.psum_pool(name="acc", bufs=4))
        ps_pool = ctx.enter_context(tc.psum_pool(name="ps", bufs=1))
        ctx.enter_context(tc.manual_schedule())

        bias_rows = keep.tile([P, P], BF16)
        nc.gpsimd.memset(bias_rows[:], 0.0)
        w1_raw = [keep.tile([P, PACK, KF], BF16, name="w1_raw%d" % g) for g in range(passes)]
        w2_raw = [keep.tile([P, PACK, W2_LOAD], BF16, name="w2_raw%d" % i) for i in range(w2_loads)]
        h_sb = keep.tile([P, D], BF16)
        logits_sb = keep.tile([P, V], BF16)
        w1_view = W_f1.rearrange("(g p j) c -> g p j c", p=P, j=PACK)
        w2_view = W_f2.rearrange("(t p) n -> p t n", p=P)
        nc.sync.dma_start(out=w1_raw[0][:], in_=w1_view[0])
        nc.sync.dma_start(out=bias_rows[0:4, :], in_=b_f1.rearrange("(t m) -> t m", m=P))
        nc.sync.dma_start(out=bias_rows[4:12, :], in_=b_f2.rearrange("(c m) -> c m", m=P))
        nc.sync.dma_start(out=h_sb[:], in_=h_dram)
        nc.sync.dma_start(out=w1_raw[1][:], in_=w1_view[1])
        for i in range(w2_loads):
            nc.sync.dma_start(out=w2_raw[i][:], in_=w2_view[:, :, i * W2_LOAD : (i + 1) * W2_LOAD])
        nc.sync.dma_start(out=logits_sb[:], in_=logits_dram)

        zeros_f32 = keep.tile([P, P], F32)
        nc.vector.memset(zeros_f32[:], 0.0)
        warm_in = keep.tile([P, 1], F32)
        warm_out = keep.tile([P, 1], F32)
        nc.vector.memset(warm_in[:], 0.0)
        nc.scalar.activation(out=warm_out[:], in_=warm_in[:], func=ACT.Gelu)

        ident_f32 = keep.tile([P, P], F32)
        ident_bf16 = keep.tile([P, P], BF16)
        make_identity(nc, ident_f32[:])
        make_identity(nc, ident_bf16[:])

        w1_grouped = [
            keep.tile([P, KF, PACK], BF16, align_bytes=64, name="w1_grouped%d" % g)
            for g in range(passes)
        ]
        w1_codes = [
            keep.tile([P, KF], U32, align_bytes=64, name="w1_codes%d" % g) for g in range(passes)
        ]
        w1_scales = [
            keep.tile([P, KF], U8, align_bytes=64, name="w1_scales%d" % g) for g in range(passes)
        ]
        halves = [slice(i * KF // 2, (i + 1) * KF // 2) for i in range(2)]

        def regroup_w1(g, i):
            cols = halves[i]
            share = W1_VECTOR_SHARE[g][i]
            regroup(nc, w1_grouped[g][:, cols, :], w1_raw[g][:, :, cols], share)

        def quantise_w1(g, i):
            cols = halves[i]
            quantise(nc, w1_codes[g][:, cols], w1_scales[g][:, cols], w1_grouped[g][:, cols, :])

        def warm(warm_ps, warm_passes, width):
            for n in range(warm_passes):
                nc.tensor.matmul_mx(
                    out=warm_ps[:, 0:width],
                    lhsT=w1_codes[0][:, 0:P].bitcast(FP8X4),
                    lhsT_scale=w1_scales[0][:, 0:P],
                    rhs=w1_codes[0][:, 0:width].bitcast(FP8X4),
                    rhs_scale=w1_scales[0][:, 0:width],
                    start=(n == 0),
                    stop=(n == warm_passes - 1),
                )

        regroup_w1(0, 0)
        regroup_w1(0, 1)

        first_warm_ps = ps_pool.tile([P, P], F32, tag="gate", bufs=3)
        for n in range(FIRST_WARM_PASSES):
            nc.tensor.matmul(
                out=first_warm_ps[:], lhsT=zeros_f32[:], rhs=zeros_f32[:],
                start=(n == 0), stop=(n == FIRST_WARM_PASSES - 1),
            )
        bias_ps = acc_pool.tile([P, P], BF16, tag="acc")
        nc.tensor.transpose(bias_ps[:], bias_rows[:], ident_bf16[:])
        b1_col = keep.tile([P, 4], F32)
        b2_half = keep.tile([P, 8], F32)
        nc.vector.tensor_copy(out=b1_col[:], in_=bias_ps[:, 0:4])
        nc.vector.tensor_scalar_mul(out=b2_half[:], in0=bias_ps[:, 4:12], scalar1=0.5)

        h_words = h_sb[:].bitcast(F32).rearrange("r (g q u) -> r g u q", g=passes, u=2)
        h_grouped = keep.tile([P, passes * P * PACK], BF16, align_bytes=64)
        h_grouped_words = h_grouped[:].bitcast(F32).rearrange("p (g r u) -> p g r u", g=passes, u=2)
        for g in range(passes):
            if g == 0:
                hT_ps = ps_pool.tile([P, 2, P], F32, tag="hT_ps")
            else:
                hT_ps = ps_pool.tile([P, 2, P], F32, tag="gate", bufs=3)
            for u in range(2):
                nc.tensor.transpose(hT_ps[:, u, :], h_words[:, g, u, :], ident_f32[:])
            nc.scalar.copy(
                out=h_grouped_words[:, g, :, :], in_=hT_ps[:].rearrange("p u r -> p r u")
            )
        h_codes = keep.tile([P, passes, P], U32, align_bytes=64)
        h_scales = keep.tile([P, passes, P], U8, align_bytes=64)

        quantise_w1(0, 0)
        early_warm_ps = ps_pool.tile([P, KF], F32, tag="gate", bufs=3)
        warm(early_warm_ps, EARLY_WARM_PASSES, KF // 2)
        quantise_w1(0, 1)
        regroup_w1(1, 0)
        regroup_w1(1, 1)
        nc.vector.quantize_mx(
            out=h_codes[:].rearrange("p g r -> p (g r)").bitcast(FP8X4),
            scales=h_scales[:].rearrange("p g r -> p (g r)"),
            in_=h_grouped[:],
        )
        quantise_w1(1, 0)
        quantise_w1(1, 1)

        hid_ps = [acc_pool.tile([P, P], F32, tag="acc", name="hid_ps%d" % t) for t in range(PACK)]
        for g in range(passes):
            for t in range(PACK):
                m_cols = slice(t * P, (t + 1) * P)
                nc.tensor.matmul_mx(
                    out=hid_ps[t][:],
                    lhsT=w1_codes[g][:, m_cols].bitcast(FP8X4),
                    lhsT_scale=w1_scales[g][:, m_cols],
                    rhs=h_codes[:, g, :].bitcast(FP8X4),
                    rhs_scale=h_scales[:, g, :],
                    start=(g == 0),
                    stop=(g == passes - 1),
                )

        late_warm_ps = ps_pool.tile([P, KF], F32, tag="hT_ps")
        warm(late_warm_ps, WARM_PASSES, KF)

        w2_grouped = [
            keep.tile([P, W2_PIECE, PACK], BF16, align_bytes=64, name="w2_grouped%d" % i)
            for i in range(w2_pieces)
        ]
        w2_codes = [
            keep.tile([P, W2_PIECE], U32, align_bytes=64, name="w2_codes%d" % i)
            for i in range(w2_pieces)
        ]
        w2_scales = [
            keep.tile([P, W2_PIECE], U8, align_bytes=64, name="w2_scales%d" % i)
            for i in range(w2_pieces)
        ]

        def regroup_w2(i):
            first = (i % pieces_per_load) * W2_PIECE
            raw = w2_raw[i // pieces_per_load][:, :, first : first + W2_PIECE]
            regroup(nc, w2_grouped[i][:], raw, W2_VECTOR_SHARE[i])

        def quantise_w2(i):
            quantise(nc, w2_codes[i][:], w2_scales[i][:], w2_grouped[i][:])

        for i in range(pieces_per_load):
            regroup_w2(i)
        quantise_w2(0)

        hid_planes = keep.tile([P, PACK, P], BF16)
        for t in range(PACK):
            nc.scalar.activation(
                out=hid_planes[:, t, :], in_=hid_ps[t][:], func=ACT.Gelu,
                bias=b1_col[:, t : t + 1], scale=1.0,
            )
        regroup_w2(2)
        hid_grouped = keep.tile([P, P, PACK], BF16, align_bytes=64)
        nc.vector.tensor_copy(
            out=hid_grouped[:].rearrange("p (c i) t -> p c t i", i=RUN),
            in_=hid_planes[:].rearrange("p t (c i) -> p c t i", i=RUN),
        )
        regroup_w2(3)
        hid_codes = keep.tile([P, P], U32, align_bytes=64)
        hid_scales = keep.tile([P, P], U8, align_bytes=64)
        quantise(nc, hid_codes[:], hid_scales[:], hid_grouped[:])

        quantise_w2(1)
        quantise_w2(2)
        quantise_w2(3)

        half_logits = keep.tile([P, V], BF16)
        nc.vector.tensor_scalar_mul(out=half_logits[:], in0=logits_sb[:], scalar1=0.5)

        tanh_sb = [keep.tile([P, chunks, P], F32, name="tanh_sb%d" % i) for i in range(w2_pieces)]

        def product(i):
            z_ps = acc_pool.tile([P, chunks, P], F32, tag="acc")
            for j in range(chunks):
                v_cols = slice(j * P, (j + 1) * P)
                nc.tensor.matmul_mx(
                    out=z_ps[:, j, :],
                    lhsT=w2_codes[i][:, v_cols].bitcast(FP8X4),
                    lhsT_scale=w2_scales[i][:, v_cols],
                    rhs=hid_codes[:].bitcast(FP8X4),
                    rhs_scale=hid_scales[:],
                    start=True,
                    stop=True,
                )
            for j in range(chunks):
                c = i * chunks + j
                nc.scalar.activation(
                    out=tanh_sb[i][:, j, :], in_=z_ps[:, j, :], func=ACT.Tanh,
                    bias=b2_half[:, c : c + 1], scale=0.5,
                )

        def finish(i):
            if i == w2_pieces - 1:
                gate_ps = ps_pool.tile([P, chunks, P], F32, tag="hT_ps")
            else:
                gate_ps = ps_pool.tile([P, chunks, P], F32, tag="gate", bufs=3)
            for j in range(chunks):
                nc.tensor.transpose(gate_ps[:, j, :], tanh_sb[i][:, j, :], ident_f32[:])
            cols = slice(i * W2_PIECE, (i + 1) * W2_PIECE)
            out_sb = keep.tile([P, W2_PIECE], F32, name="out_sb%d" % i)
            nc.vector.scalar_tensor_tensor(
                out=out_sb[:],
                in0=gate_ps[:].rearrange("p j v -> p (j v)"),
                scalar=3.0,
                in1=half_logits[:, cols],
                op0=ALU.add,
                op1=ALU.mult,
            )
            nc.sync.dma_start(out=out_dram[:, cols], in_=out_sb[:])

        for i in range(w2_pieces + FINISH_LAG):
            if i < w2_pieces:
                product(i)
            if i >= FINISH_LAG:
                finish(i - FINISH_LAG)
